import numpy as np
import ml_dtypes


def mxq(x, axis, fmt="e4m3"):
    dtype, down = {"e4m3": (ml_dtypes.float8_e4m3fn, 7), "e5m2": (ml_dtypes.float8_e5m2, 14)}[fmt]
    v = np.moveaxis(np.asarray(x, np.float32).astype(ml_dtypes.bfloat16).astype(np.float64), axis, -1)
    blocks = v.reshape(v.shape[:-1] + (-1, 32))
    amax = np.abs(blocks).max(-1, keepdims=True)
    byte = np.maximum(np.where(amax > 0, np.frexp(amax)[1] - 1 + 127, 0) - down, 1)
    scale = np.exp2(byte - 127.0)
    codes = (blocks / scale).astype(np.float32).astype(dtype).astype(np.float64)
    return np.moveaxis((codes * scale).reshape(v.shape), -1, axis)


WIDE = False


def mx_kscale(k):
    if not WIDE:
        return np.ones(k)
    levels = np.array([10, -10, 5, -5, 0])
    a = np.random.permutation(np.resize(levels, k // 512 * 4)).reshape(k // 512, 4)
    idx = np.arange(k)
    return np.exp2(a[idx // 512, idx % 128 // 32])


BF16 = ml_dtypes.bfloat16


def bf(x):
    return np.asarray(x, np.float32).astype(BF16)


def f64(x):
    return np.asarray(x).astype(np.float64)


B, S, D, H, KV, DH, QB = 4, 2048, 512, 2, 1, 128, 512
HALF = DH // 2
EPS = 1e-6


def rope_tables():
    inv_freq = 1.0 / (10000.0 ** (np.arange(HALF) / HALF))
    ang = np.arange(S)[:, None] * inv_freq[None, :]
    ang = np.concatenate([ang, ang], axis=-1)
    return np.sin(ang), np.cos(ang)


def rmsnorm(u, scale, shift):
    rms = np.sqrt(np.mean(u * u, axis=-1, keepdims=True) + EPS)
    return u / rms * (1.0 + scale) + shift


def apply_rope(u, sin, cos):
    rot = np.concatenate([-u[..., HALF:], u[..., :HALF]], axis=-1)
    return u * cos[None, None, :S, :] + rot * sin[None, None, :S, :]


def heads(u, n):
    return u.reshape(B, S, n, DH).transpose(0, 2, 1, 3)


def setup_inputs():
    s = mx_kscale(D)
    sin, cos = rope_tables()
    return {"x": bf(np.random.standard_normal((B, S, D)) * s),
            "sin_thetas": bf(sin), "cos_thetas": bf(cos),
            "wq": bf(np.random.standard_normal((H * DH, D)) / np.sqrt(D) / s),
            "wk": bf(np.random.standard_normal((KV * DH, D)) / np.sqrt(D) / s),
            "wv": bf(np.random.standard_normal((KV * DH, D)) * 2.0 / np.sqrt(D) / s),
            "q_scale": bf(np.random.standard_normal(DH) * 0.1), "q_shift": bf(np.random.standard_normal(DH) * 0.1),
            "k_scale": bf(np.random.standard_normal(DH) * 0.1), "k_shift": bf(np.random.standard_normal(DH) * 0.1)}


def reference(x, sin_thetas, cos_thetas, wq, wk, wv, q_scale, q_shift, k_scale, k_shift):
    xq = mxq(f64(x), 2, "e4m3")
    q = heads(xq @ mxq(f64(wq), 1, "e4m3").T, H)
    k = heads(xq @ mxq(f64(wk), 1, "e4m3").T, KV)
    v = heads(xq @ mxq(f64(wv), 1, "e4m3").T, KV)
    q = rmsnorm(q, f64(q_scale), f64(q_shift))
    k = rmsnorm(k, f64(k_scale), f64(k_shift))
    q = apply_rope(q, f64(sin_thetas), f64(cos_thetas))
    k = apply_rope(k, f64(sin_thetas), f64(cos_thetas))
    return q, k, v

@@ -1,0 +1,333 @@
+from contextlib import ExitStack
+
+import concourse.mybir as mybir
+from concourse.masks import make_identity
+
+F32 = mybir.dt.float32
+BF16 = mybir.dt.bfloat16
+U32 = mybir.dt.uint32
+U8 = mybir.dt.uint8
+FP8X4 = mybir.dt.float8_e4m3fn_x4
+ALU = mybir.AluOpType
+ACT = mybir.ActivationFunctionType
+
+B, S, D = 4, 2048, 512
+P = 128
+DH = 128
+HALF = DH // 2
+NT = 4
+GROUP = P * NT
+PG = S // GROUP
+NH = 3
+EPS = 1e-6
+FLOPS = 2 * B * S * D * 512
+
+
+def tile_groupqueryattention_pa_t_kernel(
+    tc, x, sin_thetas, cos_thetas, wq, wk, wv, q_scale, q_shift, k_scale, k_shift, out_0, out_1, out_2
+):
+    nc = tc.nc
+    with ExitStack() as ctx:
+        const = ctx.enter_context(tc.tile_pool(name="const", bufs=1))
+        xpool = ctx.enter_context(tc.tile_pool(name="xpool", bufs=1))
+        tabs = ctx.enter_context(tc.tile_pool(name="tabs", bufs=1))
+        work = ctx.enter_context(tc.tile_pool(name="work", bufs=2))
+        deep = ctx.enter_context(tc.tile_pool(name="deep", bufs=3))
+        psum_t = ctx.enter_context(tc.psum_pool(name="psum_t", bufs=2))
+        psum_u = ctx.enter_context(tc.psum_pool(name="psum_u", bufs=4))
+        psum_c = ctx.enter_context(tc.psum_pool(name="psum_c", bufs=2))
+        ctx.enter_context(tc.manual_schedule())
+
+        order = [(pg, b) for pg in range(PG) for b in range(B)]
+
+        ident_f = const.tile([P, P], F32, name="ident_f")
+        make_identity(nc, ident_f[:])
+
+        def load_x(gi):
+            pg, b = order[gi]
+            xs = xpool.tile([P, NT, D], BF16, name="xs%d" % gi)
+            nc.sync.dma_start(
+                out=xs[:].rearrange("p n k -> p (n k)"),
+                in_=x[b, pg * GROUP:(pg + 1) * GROUP, :].rearrange("(p n) k -> p (n k)", n=NT),
+            )
+            x_sb.append(xs)
+
+        def load_cs(eng, pg):
+            for c, tab in enumerate((cos_thetas, sin_thetas)):
+                eng.dma_start(
+                    out=cs_sb[:, c, pg * NT:(pg + 1) * NT, :],
+                    in_=tab[pg * GROUP:(pg + 1) * GROUP, :].rearrange("(p n) j -> p n j", n=NT),
+                )
+
+        x_sb = []
+        w_sb = const.tile([P, NT, D], BF16, name="w_sb")
+        vb = const.tile([P, 4, DH], BF16, name="vb")
+        cs_sb = const.tile([P, 2, PG * NT, DH], BF16, name="cs_sb")
+        nc.sync.dma_start(out=w_sb[:, 0:2, :], in_=wq.rearrange("(r p) k -> p r k", p=P))
+        nc.sync.dma_start(out=w_sb[:, 2, :], in_=wk)
+        nc.sync.dma_start(out=w_sb[:, 3, :], in_=wv)
+        load_x(0)
+        for i, vec in enumerate((q_scale, k_scale, q_shift, k_shift)):
+            nc.scalar.dma_start(out=vb[:, i, :], in_=vec.partition_broadcast(P))
+        load_cs(nc.gpsimd, 0)
+        load_x(1)
+        load_cs(nc.sync, 1)
+        load_x(2)
+        load_x(3)
+        load_cs(nc.sync, 2)
+        load_x(4)
+        load_x(5)
+        load_cs(nc.sync, 3)
+        for gi in range(6, len(order)):
+            load_x(gi)
+
+        eps_t = const.tile([P, 1], F32, name="eps_t")
+        nc.vector.memset(eps_t[:], EPS)
+        warm = const.tile([P, 1], F32, name="warm")
+        nc.scalar.activation(out=warm[:], in_=eps_t[:], func=ACT.Sqrt)
+
+        ident_b = const.tile([P, P], BF16, name="ident_b")
+        nc.vector.tensor_copy(out=ident_b[:], in_=ident_f[:])
+
+        g3 = const.tile([P, NH, DH], F32, name="g3")
+        nc.vector.tensor_scalar_add(out=g3[:, 0:2, :], in0=vb[:, 0:1, :].to_broadcast([P, 2, DH]), scalar1=1.0)
+        nc.vector.tensor_scalar_add(out=g3[:, 2, :], in0=vb[:, 1, :], scalar1=1.0)
+        gs3 = const.tile([P, NH, DH], F32, name="gs3")
+        nc.vector.tensor_copy(out=gs3[:, :, 0:HALF], in_=g3[:, :, 0:HALF])
+        nc.vector.tensor_scalar_mul(out=gs3[:, :, HALF:], in0=g3[:, :, HALF:], scalar1=-1.0)
+
+        dc = const.tile([P, 2, DH], BF16, name="dc")
+        nc.vector.tensor_tensor(
+            out=dc[:], in0=vb[:, 2:4, :], in1=ident_b[:].unsqueeze(1).to_broadcast([P, 2, DH]), op=ALU.mult
+        )
+        ds = const.tile([P, 2, DH], BF16, name="ds")
+        nc.vector.scalar_tensor_tensor(
+            out=ds[:, :, 0:HALF], in0=vb[:, 2:4, HALF:], scalar=-1.0,
+            in1=ident_b[:, 0:HALF].unsqueeze(1).to_broadcast([P, 2, HALF]), op0=ALU.mult, op1=ALU.mult,
+        )
+        nc.vector.tensor_tensor(
+            out=ds[:, :, HALF:], in0=vb[:, 2:4, 0:HALF],
+            in1=ident_b[:, HALF:].unsqueeze(1).to_broadcast([P, 2, HALF]), op=ALU.mult,
+        )
+
+        NG = len(order)
+        w_codes = const.tile([P, NT * P], U32, name="w_codes", align_bytes=64)
+        w_scales = const.tile([P, NT * P], U8, name="w_scales", align_bytes=64)
+        state = {}
+        g12_tiles = {}
+        cst_tiles = {}
+        c_tiles = {}
+
+        def transpose_group(src):
+            grouped = work.tile([P, NT, P, 4], BF16, tag="grouped", name="grouped", align_bytes=64)
+            gwords = grouped[:].bitcast(F32)
+            banks = []
+            for half in range(2):
+                xt = psum_t.tile([P, 2, 2, P], F32, tag="xt", name="xt")
+                for i in range(2):
+                    words = src[:, 2 * half + i, :].bitcast(F32)
+                    for u in range(2):
+                        nc.tensor.transpose(xt[:, i, u, :], words[:, u * P:(u + 1) * P], ident_f[:])
+                banks.append(xt)
+            for half in range(2):
+                nc.scalar.copy(
+                    out=gwords[:, 2 * half:2 * half + 2, :, :], in_=banks[half][:].rearrange("p i u r -> p i r u")
+                )
+            return grouped
+
+        def quantise(grouped, codes, scales):
+            nc.vector.quantize_mx(
+                out=codes[:].bitcast(FP8X4), scales=scales[:], in_=grouped[:].rearrange("p n r t -> p (n r t)")
+            )
+
+        def table_g1(eng, pg, n0, n1):
+            g12 = g12_tiles[pg]
+            k = n1 - n0
+            cosv = cs_sb[:, 0, pg * NT + n0:pg * NT + n1, :]
+            eng.tensor_tensor(
+                out=g12[:, n0:n1, 0, :, :], in0=cosv.unsqueeze(2).to_broadcast([P, k, NH, DH]),
+                in1=g3[:].unsqueeze(1).to_broadcast([P, k, NH, DH]), op=ALU.mult,
+            )
+
+        def table_g2(eng, pg, n0, n1, c):
+            g12 = g12_tiles[pg]
+            k = n1 - n0
+            sinv = cs_sb[:, 1, pg * NT + n0:pg * NT + n1, (1 - c) * HALF:(2 - c) * HALF]
+            eng.tensor_tensor(
+                out=g12[:, n0:n1, 1, :, c * HALF:(c + 1) * HALF],
+                in0=sinv.unsqueeze(2).to_broadcast([P, k, NH, HALF]),
+                in1=gs3[:, :, c * HALF:(c + 1) * HALF].unsqueeze(1).to_broadcast([P, k, NH, HALF]), op=ALU.mult,
+            )
+
+        def table_t(pg):
+            cst_ps = psum_t.tile([P, 2, NT, P], BF16, tag="xt", name="cst_ps")
+            for c in range(2):
+                for n in range(NT):
+                    nc.tensor.transpose(cst_ps[:, c, n, :], cs_sb[:, c, pg * NT + n, :], ident_b[:])
+            cst = work.tile([P, 2, NT, P], BF16, tag="cst", name="cst")
+            nc.scalar.copy(out=cst[:], in_=cst_ps[:])
+            cst_tiles[pg] = cst
+
+        def table_c(pg):
+            cst = cst_tiles[pg]
+            pair = []
+            for half in range(2):
+                c_ps = psum_c.tile([P, 2, 2, DH], F32, tag="c", name="c_ps")
+                for i in range(2):
+                    n = 2 * half + i
+                    dst = c_ps[:, i, :, :].rearrange("p a j -> p (a j)")
+                    nc.tensor.matmul(
+                        dst, lhsT=cst[:, 0, n, :], rhs=dc[:].rearrange("p a j -> p (a j)"), start=True, stop=False
+                    )
+                    nc.tensor.matmul(
+                        dst, lhsT=cst[:, 1, n, :], rhs=ds[:].rearrange("p a j -> p (a j)"), start=False, stop=True
+                    )
+                pair.append(c_ps)
+            c_tiles[pg] = pair
+
+        def front(gi):
+            state[gi] = {"grouped": transpose_group(x_sb[gi])}
+
+        def quant(gi):
+            st = state[gi]
+            st["codes"] = deep.tile([P, NT * P], U32, tag="codes", name="codes", align_bytes=64)
+            st["scales"] = deep.tile([P, NT * P], U8, tag="scales", name="scales", align_bytes=64)
+            quantise(st["grouped"], st["codes"], st["scales"])
+
+        def project(gi, n):
+            st = state[gi]
+            if n == 0:
+                st["ss"] = deep.tile([P, NT * NH], F32, tag="ss", name="ss")
+                st["ov"] = deep.tile([P, NT, DH], F32, tag="ov", name="ov")
+                st["u"] = []
+            codes, scales, ss, ov = st["codes"], st["scales"], st["ss"], st["ov"]
+            u = psum_u.tile([P, 4 * DH], F32, tag="u", name="u")
+            st["u"].append(u)
+            nc.tensor.matmul_mx(
+                out=u[:],
+                lhsT=codes[:, n * P:(n + 1) * P].bitcast(FP8X4),
+                lhsT_scale=scales[:, n * P:(n + 1) * P],
+                rhs=w_codes[:].bitcast(FP8X4),
+                rhs_scale=w_scales[:],
+                start=True,
+                stop=True,
+            )
+            for h in range(NH):
+                junk = work.tile([P, DH], BF16, tag="junk", name="junk")
+                nc.scalar.activation(
+                    out=junk[:], in_=u[:, h * DH:(h + 1) * DH], func=ACT.Square,
+                    accum_out=ss[:, n * NH + h:n * NH + h + 1],
+                )
+            nc.scalar.copy(out=ov[:, n, :], in_=u[:, NH * DH:])
+
+        def norm_root(gi):
+            pg, b = order[gi]
+            st = state[gi]
+            st["rms"] = deep.tile([P, NT * NH], F32, tag="rms", name="rms")
+            nc.scalar.activation(out=st["rms"][:], in_=st["ss"][:], func=ACT.Sqrt, scale=1.0 / DH, bias=eps_t[:])
+            lo = pg * GROUP
+            nc.sync.dma_start(
+                out=out_2[b, 0, lo:lo + GROUP, :].rearrange("(p n) j -> p (n j)", n=NT),
+                in_=st["ov"][:].rearrange("p n j -> p (n j)"),
+            )
+
+        def products(gi, n):
+            pg, b = order[gi]
+            st = state[gi]
+            if n == 0:
+                st["t12"] = deep.tile([P, NT, 2, NH, 2, HALF], F32, tag="t12", name="t12")
+            u = st["u"][n]
+            nc.vector.tensor_tensor(
+                out=st["t12"][:, n, :, :, :, :].rearrange("p a h c j -> p a (h c j)"),
+                in0=u[:, 0:NH * DH].unsqueeze(1).to_broadcast([P, 2, NH * DH]),
+                in1=g12_tiles[pg][:, n, :, :, :].rearrange("p a h j -> p a (h j)"),
+                op=ALU.mult,
+            )
+
+        def join(gi, half):
+            t12 = state[gi]["t12"]
+            n0, n1 = 2 * half, 2 * half + 2
+            for c in range(2):
+                nc.gpsimd.tensor_tensor(
+                    out=t12[:, n0:n1, 0, :, c, :], in0=t12[:, n0:n1, 0, :, c, :],
+                    in1=t12[:, n0:n1, 1, :, 1 - c, :], op=ALU.add,
+                )
+
+        def norm_recip(gi):
+            st = state[gi]
+            st["rinv"] = deep.tile([P, NT * NH], F32, tag="rinv", name="rinv")
+            nc.vector.reciprocal(out=st["rinv"][:], in_=st["rms"][:])
+
+        def finish(gi):
+            pg, b = order[gi]
+            st = state[gi]
+            t12, rinv = st["t12"], st["rinv"]
+            oqk = deep.tile([P, NH, NT, DH], F32, tag="oqk", name="oqk")
+            for n in range(NT):
+                c_ps = c_tiles[pg][n // 2]
+                for h in range(NH):
+                    nc.vector.scalar_tensor_tensor(
+                        out=oqk[:, h, n, :],
+                        in0=t12[:, n, 0, h, :, :].rearrange("p c j -> p (c j)"),
+                        scalar=rinv[:, n * NH + h:n * NH + h + 1],
+                        in1=c_ps[:, n % 2, h // 2, :],
+                        op0=ALU.mult,
+                        op1=ALU.add,
+                    )
+            lo = pg * GROUP
+            nc.sync.dma_start(
+                out=out_0[b, :, lo:lo + GROUP, :].rearrange("h (p n) j -> p h (n j)", n=NT),
+                in_=oqk[:, 0:2, :, :].rearrange("p h n j -> p h (n j)"),
+            )
+            nc.sync.dma_start(
+                out=out_1[b, 0, lo:lo + GROUP, :].rearrange("(p n) j -> p (n j)", n=NT),
+                in_=oqk[:, 2, :, :].rearrange("p n j -> p (n j)"),
+            )
+
+        for pg in range(PG):
+            g12_tiles[pg] = tabs.tile([P, NT, 2, NH, DH], F32, name="g12_%d" % pg)
+
+        late_tables = {0: (2, 0), 1: (2, 1), 3: (2, 2), 4: (2, 3), 6: (3, 0), 7: (3, 1), 9: (3, 2), 10: (3, 3)}
+
+        def table_tile(eng, pg, n0, n1):
+            table_g1(eng, pg, n0, n1)
+            table_g2(eng, pg, n0, n1, 0)
+            table_g2(eng, pg, n0, n1, 1)
+
+        w_grouped = transpose_group(w_sb)
+        table_tile(nc.gpsimd, 0, 0, 1)
+        table_tile(nc.gpsimd, 0, 1, 2)
+        table_tile(nc.gpsimd, 1, 0, NT)
+        quantise(w_grouped, w_codes, w_scales)
+        for it in range(-2, NG + 1):
+            if it + 2 < NG:
+                front(it + 2)
+            if it == -2:
+                table_tile(nc.vector, 0, 2, 3)
+                table_t(0)
+                table_c(0)
+            for n in range(NT):
+                if 0 <= it < NG:
+                    products(it, n)
+                if 0 <= it + 1 < NG:
+                    project(it + 1, n)
+                if 0 <= it < NG and n % 2 == 1:
+                    join(it, n // 2)
+            if 0 <= it + 1 < NG:
+                norm_root(it + 1)
+            if 0 <= it < NG:
+                norm_recip(it)
+            if 0 <= it - 1:
+                finish(it - 1)
+                pg, b = order[it - 1]
+                if b == B - 1 and pg + 1 < PG:
+                    table_c(pg + 1)
+            if it + 2 < NG:
+                quant(it + 2)
+            if it == -2:
+                table_tile(nc.vector, 0, 3, 4)
+            if it in late_tables:
+                pg, n = late_tables[it]
+                table_tile(nc.gpsimd, pg, n, n + 1)
+            if 0 <= it < NG and order[it][1] == 1 and order[it][0] + 1 < PG:
+                table_t(order[it][0] + 1)

@@ -244,11 +244,10 @@ def tile_groupqueryattention_pa_t_kernel(
                 op=ALU.mult,
             )
 
-        def join(gi, half):
+        def join(eng, gi, n0, n1):
             t12 = state[gi]["t12"]
-            n0, n1 = 2 * half, 2 * half + 2
             for c in range(2):
-                nc.gpsimd.tensor_tensor(
+                eng.tensor_tensor(
                     out=t12[:, n0:n1, 0, :, c, :], in0=t12[:, n0:n1, 0, :, c, :],
                     in1=t12[:, n0:n1, 1, :, 1 - c, :], op=ALU.add,
                 )
@@ -289,6 +288,11 @@ def tile_groupqueryattention_pa_t_kernel(
 
         late_tables = {0: (2, 0), 1: (2, 1), 3: (2, 2), 4: (2, 3), 6: (3, 0), 7: (3, 1), 9: (3, 2), 10: (3, 3)}
 
+        def pool_banks(it):
+            if it == NG - 1:
+                return 0
+            return 2 if it in late_tables else 3
+
         def table_tile(eng, pg, n0, n1):
             table_g1(eng, pg, n0, n1)
             table_g2(eng, pg, n0, n1, 0)
@@ -311,8 +315,10 @@ def tile_groupqueryattention_pa_t_kernel(
                     products(it, n)
                 if 0 <= it + 1 < NG:
                     project(it + 1, n)
-                if 0 <= it < NG and n % 2 == 1:
-                    join(it, n // 2)
+                if 0 <= it < NG and n + 1 == pool_banks(it):
+                    join(nc.gpsimd, it, 0, n + 1)
+            if 0 <= it < NG and pool_banks(it) < NT:
+                join(nc.vector, it, pool_banks(it), NT)
             if 0 <= it + 1 < NG:
                 norm_root(it + 1)
             if 0 <= it < NG:

@@ -262,6 +262,7 @@ def tile_groupqueryattention_pa_t_kernel(
             st = state[gi]
             t12, rinv = st["t12"], st["rinv"]
             oqk = deep.tile([P, NH, NT, DH], F32, tag="oqk", name="oqk")
+            st["oqk"] = oqk
             for n in range(NT):
                 c_ps = c_tiles[pg][n // 2]
                 for h in range(NH):
@@ -288,20 +289,25 @@ def tile_groupqueryattention_pa_t_kernel(
 
         late_tables = {0: (2, 0), 1: (2, 1), 3: (2, 2), 4: (2, 3), 6: (3, 0), 7: (3, 1), 9: (3, 2), 10: (3, 3)}
 
-        def pool_banks(it):
-            if it == NG - 1:
+        def pool_banks(gi):
+            if gi == 0 or gi == NG - 1:
                 return 0
-            return 2 if it in late_tables else 3
+            return 3
 
         def table_tile(eng, pg, n0, n1):
             table_g1(eng, pg, n0, n1)
             table_g2(eng, pg, n0, n1, 0)
             table_g2(eng, pg, n0, n1, 1)
 
+        def hold_pool(gi):
+            hold = work.tile([P, 1], F32, tag="hold", name="hold")
+            nc.gpsimd.tensor_copy(out=hold[:], in_=state[gi]["oqk"][:, NH - 1, NT - 1, DH - 1:DH])
+
         w_grouped = transpose_group(w_sb)
         table_tile(nc.gpsimd, 0, 0, 1)
         table_tile(nc.gpsimd, 0, 1, 2)
-        table_tile(nc.gpsimd, 1, 0, NT)
+        for n in range(NT):
+            table_tile(nc.gpsimd, 1, n, n + 1)
         quantise(w_grouped, w_codes, w_scales)
         for it in range(-2, NG + 1):
             if it + 2 < NG:
@@ -310,30 +316,31 @@ def tile_groupqueryattention_pa_t_kernel(
                 table_tile(nc.vector, 0, 2, 3)
                 table_t(0)
                 table_c(0)
+            if 0 <= it - 1 and pool_banks(it - 1) > 0:
+                hold_pool(it - 2)
+                join(nc.gpsimd, it - 1, 0, pool_banks(it - 1))
             for n in range(NT):
                 if 0 <= it < NG:
                     products(it, n)
                 if 0 <= it + 1 < NG:
                     project(it + 1, n)
-                if 0 <= it < NG and n + 1 == pool_banks(it):
-                    join(nc.gpsimd, it, 0, n + 1)
-            if 0 <= it < NG and pool_banks(it) < NT:
-                join(nc.vector, it, pool_banks(it), NT)
             if 0 <= it + 1 < NG:
                 norm_root(it + 1)
             if 0 <= it < NG:
                 norm_recip(it)
-            if 0 <= it - 1:
-                finish(it - 1)
-                pg, b = order[it - 1]
-                if b == B - 1 and pg + 1 < PG:
-                    table_c(pg + 1)
             if it + 2 < NG:
                 quant(it + 2)
             if it == -2:
                 table_tile(nc.vector, 0, 3, 4)
             if it in late_tables:
                 pg, n = late_tables[it]
-                table_tile(nc.gpsimd, pg, n, n + 1)
+                table_tile(nc.vector, pg, n, n + 1)
+            if 0 <= it - 1:
+                if pool_banks(it - 1) < NT:
+                    join(nc.vector, it - 1, pool_banks(it - 1), NT)
+                finish(it - 1)
+                pg, b = order[it - 1]
+                if b == B - 1 and pg + 1 < PG:
+                    table_c(pg + 1)
             if 0 <= it < NG and order[it][1] == 1 and order[it][0] + 1 < PG:
                 table_t(order[it][0] + 1)

@@ -33,6 +33,7 @@ def tile_groupqueryattention_pa_t_kernel(
         tabs = ctx.enter_context(tc.tile_pool(name="tabs", bufs=1))
         work = ctx.enter_context(tc.tile_pool(name="work", bufs=2))
         deep = ctx.enter_context(tc.tile_pool(name="deep", bufs=3))
+        single = ctx.enter_context(tc.tile_pool(name="single", bufs=1))
         psum_t = ctx.enter_context(tc.psum_pool(name="psum_t", bufs=2))
         psum_u = ctx.enter_context(tc.psum_pool(name="psum_u", bufs=4))
         psum_c = ctx.enter_context(tc.psum_pool(name="psum_c", bufs=2))
@@ -84,10 +85,13 @@ def tile_groupqueryattention_pa_t_kernel(
         eps_t = const.tile([P, 1], F32, name="eps_t")
         nc.vector.memset(eps_t[:], EPS)
         warm = const.tile([P, 1], F32, name="warm")
-        nc.scalar.activation(out=warm[:], in_=eps_t[:], func=ACT.Sqrt)
+        nc.scalar.activation(out=warm[:], in_=eps_t[:], func=ACT.Abs_reciprocal_sqrt)
 
         ident_b = const.tile([P, P], BF16, name="ident_b")
         nc.vector.tensor_copy(out=ident_b[:], in_=ident_f[:])
+        perm_f = const.tile([P, P], F32, name="perm_f")
+        nc.vector.tensor_copy(out=perm_f[:, 0:HALF], in_=ident_f[:, HALF:])
+        nc.vector.tensor_copy(out=perm_f[:, HALF:], in_=ident_f[:, 0:HALF])
 
         g3 = const.tile([P, NH, DH], F32, name="g3")
         nc.vector.tensor_scalar_add(out=g3[:, 0:2, :], in0=vb[:, 0:1, :].to_broadcast([P, 2, DH]), scalar1=1.0)
@@ -97,18 +101,29 @@ def tile_groupqueryattention_pa_t_kernel(
         nc.vector.tensor_scalar_mul(out=gs3[:, :, HALF:], in0=g3[:, :, HALF:], scalar1=-1.0)
 
         dc = const.tile([P, 2, DH], BF16, name="dc")
-        nc.vector.tensor_tensor(
-            out=dc[:], in0=vb[:, 2:4, :], in1=ident_b[:].unsqueeze(1).to_broadcast([P, 2, DH]), op=ALU.mult
-        )
         ds = const.tile([P, 2, DH], BF16, name="ds")
-        nc.vector.scalar_tensor_tensor(
-            out=ds[:, :, 0:HALF], in0=vb[:, 2:4, HALF:], scalar=-1.0,
-            in1=ident_b[:, 0:HALF].unsqueeze(1).to_broadcast([P, 2, HALF]), op0=ALU.mult, op1=ALU.mult,
-        )
-        nc.vector.tensor_tensor(
-            out=ds[:, :, HALF:], in0=vb[:, 2:4, 0:HALF],
-            in1=ident_b[:, HALF:].unsqueeze(1).to_broadcast([P, 2, HALF]), op=ALU.mult,
-        )
+        bsrc = const.tile([P, 4, DH], F32, name="bsrc")
+        colv = const.tile([P, 4], F32, name="colv")
+
+        def small_tables():
+            nc.vector.tensor_tensor(
+                out=dc[:], in0=vb[:, 2:4, :], in1=ident_b[:].unsqueeze(1).to_broadcast([P, 2, DH]), op=ALU.mult
+            )
+            nc.vector.scalar_tensor_tensor(
+                out=ds[:, :, 0:HALF], in0=vb[:, 2:4, HALF:], scalar=-1.0,
+                in1=ident_b[:, 0:HALF].unsqueeze(1).to_broadcast([P, 2, HALF]), op0=ALU.mult, op1=ALU.mult,
+            )
+            nc.vector.tensor_tensor(
+                out=ds[:, :, HALF:], in0=vb[:, 2:4, 0:HALF],
+                in1=ident_b[:, HALF:].unsqueeze(1).to_broadcast([P, 2, HALF]), op=ALU.mult,
+            )
+            nc.vector.tensor_copy(out=bsrc[:, 0:2, :], in_=g3[:, 1:3, :])
+            nc.vector.tensor_copy(out=bsrc[:, 2:4, 0:HALF], in_=gs3[:, 1:3, HALF:])
+            nc.vector.tensor_copy(out=bsrc[:, 2:4, HALF:], in_=gs3[:, 1:3, 0:HALF])
+            col_ps = psum_t.tile([P, 4, P], F32, tag="xt", name="col_ps")
+            for i in range(4):
+                nc.tensor.transpose(col_ps[:, i, :], bsrc[:, i, :], ident_f[:])
+            nc.scalar.copy(out=colv[:], in_=col_ps[:, :, 0])
 
         NG = len(order)
         w_codes = const.tile([P, NT * P], U32, name="w_codes", align_bytes=64)
@@ -118,7 +133,7 @@ def tile_groupqueryattention_pa_t_kernel(
         cst_tiles = {}
         c_tiles = {}
 
-        def transpose_group(src):
+        def transpose_group(src, share=False):
             grouped = work.tile([P, NT, P, 4], BF16, tag="grouped", name="grouped", align_bytes=64)
             gwords = grouped[:].bitcast(F32)
             banks = []
@@ -130,9 +145,11 @@ def tile_groupqueryattention_pa_t_kernel(
                         nc.tensor.transpose(xt[:, i, u, :], words[:, u * P:(u + 1) * P], ident_f[:])
                 banks.append(xt)
             for half in range(2):
-                nc.scalar.copy(
-                    out=gwords[:, 2 * half:2 * half + 2, :, :], in_=banks[half][:].rearrange("p i u r -> p i r u")
-                )
+                dst = gwords[:, 2 * half:2 * half + 2, :, :]
+                if share and half == 1:
+                    nc.vector.tensor_copy(out=dst, in_=banks[half][:].rearrange("p i u r -> p i r u"))
+                else:
+                    nc.scalar.copy(out=dst, in_=banks[half][:].rearrange("p i u r -> p i r u"))
             return grouped
 
         def quantise(grouped, codes, scales):
@@ -186,7 +203,30 @@ def tile_groupqueryattention_pa_t_kernel(
             c_tiles[pg] = pair
 
         def front(gi):
-            state[gi] = {"grouped": transpose_group(x_sb[gi])}
+            state[gi] = {"grouped": transpose_group(x_sb[gi], share=(gi < 2))}
+
+        def table_front(pg, n):
+            if n == 0:
+                cst_tiles[pg] = work.tile([P, 2, NT, P], BF16, tag="cst", name="cst")
+            cs_ps = psum_t.tile([P, 2, P], BF16, tag="xt", name="cs_ps")
+            for c in range(2):
+                nc.tensor.transpose(cs_ps[:, c, :], cs_sb[:, c, pg * NT + n, :], ident_b[:])
+            nc.scalar.copy(out=cst_tiles[pg][:, :, n, :], in_=cs_ps[:])
+            xs4 = work.tile([P, 4, P], F32, tag="xs4", name="xs4")
+            for i in range(4):
+                nc.scalar.activation(
+                    out=xs4[:, i, :], in_=cs_ps[:, i // 2, :], func=ACT.Copy, scale=colv[:, i:i + 1]
+                )
+            return xs4
+
+        def table_back(pg, n, xs4):
+            gt = psum_t.tile([P, 2, 2, P], F32, tag="xt", name="gt")
+            for a in range(2):
+                for qk in range(2):
+                    nc.tensor.transpose(gt[:, a, qk, :], xs4[:, 2 * a + qk, :], ident_f[:] if a == 0 else perm_f[:])
+            g12 = g12_tiles[pg]
+            nc.scalar.copy(out=g12[:, n, :, 0:2, :], in_=gt[:, :, 0:1, :].to_broadcast([P, 2, 2, DH]))
+            nc.scalar.copy(out=g12[:, n, :, 2, :], in_=gt[:, :, 1, :])
 
         def quant(gi):
             st = state[gi]
@@ -223,8 +263,10 @@ def tile_groupqueryattention_pa_t_kernel(
         def norm_root(gi):
             pg, b = order[gi]
             st = state[gi]
-            st["rms"] = deep.tile([P, NT * NH], F32, tag="rms", name="rms")
-            nc.scalar.activation(out=st["rms"][:], in_=st["ss"][:], func=ACT.Sqrt, scale=1.0 / DH, bias=eps_t[:])
+            st["rinv"] = deep.tile([P, NT * NH], F32, tag="rinv", name="rinv")
+            nc.scalar.activation(
+                out=st["rinv"][:], in_=st["ss"][:], func=ACT.Abs_reciprocal_sqrt, scale=1.0 / DH, bias=eps_t[:]
+            )
             lo = pg * GROUP
             nc.sync.dma_start(
                 out=out_2[b, 0, lo:lo + GROUP, :].rearrange("(p n) j -> p (n j)", n=NT),
@@ -252,73 +294,72 @@ def tile_groupqueryattention_pa_t_kernel(
                     in1=t12[:, n0:n1, 1, :, 1 - c, :], op=ALU.add,
                 )
 
-        def norm_recip(gi):
+        def join_pool(gi):
             st = state[gi]
-            st["rinv"] = deep.tile([P, NT * NH], F32, tag="rinv", name="rinv")
-            nc.vector.reciprocal(out=st["rinv"][:], in_=st["rms"][:])
+            t12 = st["t12"]
+            t3 = single.tile([P, NT, NH, 2, HALF], F32, tag="t3", name="t3")
+            st["t3"] = t3
+            for n0 in (0, 2):
+                for c in range(2):
+                    nc.gpsimd.tensor_tensor(
+                        out=t3[:, n0:n0 + 2, :, c, :], in0=t12[:, n0:n0 + 2, 0, :, c, :],
+                        in1=t12[:, n0:n0 + 2, 1, :, 1 - c, :], op=ALU.add,
+                    )
 
-        def finish(gi):
+        def finish(gi, blocks):
             pg, b = order[gi]
             st = state[gi]
-            t12, rinv = st["t12"], st["rinv"]
-            oqk = deep.tile([P, NH, NT, DH], F32, tag="oqk", name="oqk")
-            st["oqk"] = oqk
-            for n in range(NT):
-                c_ps = c_tiles[pg][n // 2]
-                for h in range(NH):
-                    nc.vector.scalar_tensor_tensor(
-                        out=oqk[:, h, n, :],
-                        in0=t12[:, n, 0, h, :, :].rearrange("p c j -> p (c j)"),
-                        scalar=rinv[:, n * NH + h:n * NH + h + 1],
-                        in1=c_ps[:, n % 2, h // 2, :],
-                        op0=ALU.mult,
-                        op1=ALU.add,
-                    )
+            if "oqk" not in st:
+                st["oqk"] = deep.tile([P, NH, NT, DH], F32, tag="oqk", name="oqk")
+            for n, h in blocks:
+                summed = st["t3"][:, n, h, :, :] if "t3" in st else st["t12"][:, n, 0, h, :, :]
+                nc.vector.scalar_tensor_tensor(
+                    out=st["oqk"][:, h, n, :],
+                    in0=summed.rearrange("p c j -> p (c j)"),
+                    scalar=st["rinv"][:, n * NH + h:n * NH + h + 1],
+                    in1=c_tiles[pg][n // 2][:, n % 2, h // 2, :],
+                    op0=ALU.mult,
+                    op1=ALU.add,
+                )
+
+        def store(gi, n0, n1):
+            pg, b = order[gi]
+            oqk = state[gi]["oqk"]
             lo = pg * GROUP
             nc.sync.dma_start(
-                out=out_0[b, :, lo:lo + GROUP, :].rearrange("h (p n) j -> p h (n j)", n=NT),
-                in_=oqk[:, 0:2, :, :].rearrange("p h n j -> p h (n j)"),
+                out=out_0[b, :, lo:lo + GROUP, :].rearrange("h (p n) j -> p h n j", n=NT)[:, :, n0:n1, :],
+                in_=oqk[:, 0:2, n0:n1, :],
             )
             nc.sync.dma_start(
-                out=out_1[b, 0, lo:lo + GROUP, :].rearrange("(p n) j -> p (n j)", n=NT),
-                in_=oqk[:, 2, :, :].rearrange("p n j -> p (n j)"),
+                out=out_1[b, 0, lo:lo + GROUP, :].rearrange("(p n) j -> p n j", n=NT)[:, n0:n1, :],
+                in_=oqk[:, 2, n0:n1, :],
             )
 
         for pg in range(PG):
             g12_tiles[pg] = tabs.tile([P, NT, 2, NH, DH], F32, name="g12_%d" % pg)
-
-        late_tables = {0: (2, 0), 1: (2, 1), 3: (2, 2), 4: (2, 3), 6: (3, 0), 7: (3, 1), 9: (3, 2), 10: (3, 3)}
-
-        def pool_banks(gi):
-            if gi == 0 or gi == NG - 1:
-                return 0
-            return 3
 
         def table_tile(eng, pg, n0, n1):
             table_g1(eng, pg, n0, n1)
             table_g2(eng, pg, n0, n1, 0)
             table_g2(eng, pg, n0, n1, 1)
 
-        def hold_pool(gi):
-            hold = work.tile([P, 1], F32, tag="hold", name="hold")
-            nc.gpsimd.tensor_copy(out=hold[:], in_=state[gi]["oqk"][:, NH - 1, NT - 1, DH - 1:DH])
+        late_tables = {0: (2, 0), 1: (2, 1), 3: (2, 2), 4: (2, 3), 6: (3, 0), 7: (3, 1), 9: (3, 2), 10: (3, 3)}
+        all_blocks = [(n, h) for n in range(NT) for h in range(NH)]
 
-        w_grouped = transpose_group(w_sb)
-        table_tile(nc.gpsimd, 0, 0, 1)
-        table_tile(nc.gpsimd, 0, 1, 2)
-        for n in range(NT):
-            table_tile(nc.gpsimd, 1, n, n + 1)
+        w_grouped = transpose_group(w_sb, share=True)
+        for pg, n in ((0, 0), (0, 1), (1, 0), (1, 1)):
+            table_tile(nc.gpsimd, pg, n, n + 1)
         quantise(w_grouped, w_codes, w_scales)
         for it in range(-2, NG + 1):
             if it + 2 < NG:
                 front(it + 2)
-            if it == -2:
-                table_tile(nc.vector, 0, 2, 3)
-                table_t(0)
-                table_c(0)
-            if 0 <= it - 1 and pool_banks(it - 1) > 0:
-                hold_pool(it - 2)
-                join(nc.gpsimd, it - 1, 0, pool_banks(it - 1))
+            if it in late_tables:
+                pg, n = late_tables[it]
+                scaled = table_front(pg, n)
+            if 0 <= it - 1 < NG - 1:
+                join_pool(it - 1)
+            if it == 1 or it == 2:
+                table_tile(nc.gpsimd, 1, it + 1, it + 2)
             for n in range(NT):
                 if 0 <= it < NG:
                     products(it, n)
@@ -326,21 +367,29 @@ def tile_groupqueryattention_pa_t_kernel(
                     project(it + 1, n)
             if 0 <= it + 1 < NG:
                 norm_root(it + 1)
-            if 0 <= it < NG:
-                norm_recip(it)
-            if it + 2 < NG:
-                quant(it + 2)
-            if it == -2:
-                table_tile(nc.vector, 0, 3, 4)
             if it in late_tables:
                 pg, n = late_tables[it]
-                table_tile(nc.vector, pg, n, n + 1)
-            if 0 <= it - 1:
-                if pool_banks(it - 1) < NT:
-                    join(nc.vector, it - 1, pool_banks(it - 1), NT)
-                finish(it - 1)
+                table_back(pg, n, scaled)
+            if 0 <= it - 1 < NG - 1:
+                finish(it - 1, all_blocks[:-1])
+            if it + 2 < NG:
+                quant(it + 2)
+            if 0 <= it - 1 < NG - 1:
+                finish(it - 1, all_blocks[-1:])
+                store(it - 1, 0, NT)
                 pg, b = order[it - 1]
                 if b == B - 1 and pg + 1 < PG:
                     table_c(pg + 1)
-            if 0 <= it < NG and order[it][1] == 1 and order[it][0] + 1 < PG:
-                table_t(order[it][0] + 1)
+            if it < 0:
+                table_tile(nc.vector, 0, it + NT, it + NT + 1)
+            if it == -1:
+                small_tables()
+                table_t(0)
+                table_c(0)
+            if it == 2:
+                table_t(1)
+            if it - 1 == NG - 1:
+                for n0 in (0, 2):
+                    join(nc.vector, it - 1, n0, n0 + 2)
+                    finish(it - 1, all_blocks[n0 * NH:(n0 + 2) * NH])
+                    store(it - 1, n0, n0 + 2)

@@ -68,9 +68,9 @@ def tile_groupqueryattention_pa_t_kernel(
         nc.sync.dma_start(out=w_sb[:, 2, :], in_=wk)
         nc.sync.dma_start(out=w_sb[:, 3, :], in_=wv)
         load_x(0)
+        load_cs(nc.scalar, 0)
         for i, vec in enumerate((q_scale, k_scale, q_shift, k_shift)):
             nc.scalar.dma_start(out=vb[:, i, :], in_=vec.partition_broadcast(P))
-        load_cs(nc.gpsimd, 0)
         load_x(1)
         load_cs(nc.sync, 1)
         load_x(2)
@@ -105,6 +105,10 @@ def tile_groupqueryattention_pa_t_kernel(
         bsrc = const.tile([P, 4, DH], F32, name="bsrc")
         colv = const.tile([P, 4], F32, name="colv")
 
+        nc.vector.tensor_copy(out=bsrc[:, 0:2, :], in_=g3[:, 1:3, :])
+        nc.vector.tensor_copy(out=bsrc[:, 2:4, 0:HALF], in_=gs3[:, 1:3, HALF:])
+        nc.vector.tensor_copy(out=bsrc[:, 2:4, HALF:], in_=gs3[:, 1:3, 0:HALF])
+
         def small_tables():
             nc.vector.tensor_tensor(
                 out=dc[:], in0=vb[:, 2:4, :], in1=ident_b[:].unsqueeze(1).to_broadcast([P, 2, DH]), op=ALU.mult
@@ -117,9 +121,6 @@ def tile_groupqueryattention_pa_t_kernel(
                 out=ds[:, :, HALF:], in0=vb[:, 2:4, 0:HALF],
                 in1=ident_b[:, HALF:].unsqueeze(1).to_broadcast([P, 2, HALF]), op=ALU.mult,
             )
-            nc.vector.tensor_copy(out=bsrc[:, 0:2, :], in_=g3[:, 1:3, :])
-            nc.vector.tensor_copy(out=bsrc[:, 2:4, 0:HALF], in_=gs3[:, 1:3, HALF:])
-            nc.vector.tensor_copy(out=bsrc[:, 2:4, HALF:], in_=gs3[:, 1:3, 0:HALF])
             col_ps = psum_t.tile([P, 4, P], F32, tag="xt", name="col_ps")
             for i in range(4):
                 nc.tensor.transpose(col_ps[:, i, :], bsrc[:, i, :], ident_f[:])
@@ -132,6 +133,7 @@ def tile_groupqueryattention_pa_t_kernel(
         g12_tiles = {}
         cst_tiles = {}
         c_tiles = {}
+        cq_tiles = {}
 
         def transpose_group(src, share=False):
             grouped = work.tile([P, NT, P, 4], BF16, tag="grouped", name="grouped", align_bytes=64)
@@ -201,6 +203,9 @@ def tile_groupqueryattention_pa_t_kernel(
                     )
                 pair.append(c_ps)
             c_tiles[pg] = pair
+            cq_last = const.tile([P, DH], F32, name="cq_last%d" % pg)
+            nc.scalar.copy(out=cq_last[:], in_=pair[1][:, 1, 0, :])
+            cq_tiles[pg] = cq_last
 
         def front(gi):
             state[gi] = {"grouped": transpose_group(x_sb[gi], share=(gi < 2))}
@@ -277,10 +282,10 @@ def tile_groupqueryattention_pa_t_kernel(
             pg, b = order[gi]
             st = state[gi]
             if n == 0:
-                st["t12"] = deep.tile([P, NT, 2, NH, 2, HALF], F32, tag="t12", name="t12")
+                st["t12"] = deep.tile([P, 2, NT, NH, 2, HALF], F32, tag="t12", name="t12")
             u = st["u"][n]
             nc.vector.tensor_tensor(
-                out=st["t12"][:, n, :, :, :, :].rearrange("p a h c j -> p a (h c j)"),
+                out=st["t12"][:, :, n, :, :, :].rearrange("p a h c j -> p a (h c j)"),
                 in0=u[:, 0:NH * DH].unsqueeze(1).to_broadcast([P, 2, NH * DH]),
                 in1=g12_tiles[pg][:, n, :, :, :].rearrange("p a h j -> p a (h j)"),
                 op=ALU.mult,
@@ -290,8 +295,8 @@ def tile_groupqueryattention_pa_t_kernel(
             t12 = state[gi]["t12"]
             for c in range(2):
                 eng.tensor_tensor(
-                    out=t12[:, n0:n1, 0, :, c, :], in0=t12[:, n0:n1, 0, :, c, :],
-                    in1=t12[:, n0:n1, 1, :, 1 - c, :], op=ALU.add,
+                    out=t12[:, 0, n0:n1, :, c, :], in0=t12[:, 0, n0:n1, :, c, :],
+                    in1=t12[:, 1, n0:n1, :, 1 - c, :], op=ALU.add,
                 )
 
         def join_pool(gi):
@@ -300,11 +305,27 @@ def tile_groupqueryattention_pa_t_kernel(
             t3 = single.tile([P, NT, NH, 2, HALF], F32, tag="t3", name="t3")
             st["t3"] = t3
             for n0 in (0, 2):
-                for c in range(2):
-                    nc.gpsimd.tensor_tensor(
-                        out=t3[:, n0:n0 + 2, :, c, :], in0=t12[:, n0:n0 + 2, 0, :, c, :],
-                        in1=t12[:, n0:n0 + 2, 1, :, 1 - c, :], op=ALU.add,
-                    )
+                nc.gpsimd.tensor_tensor(
+                    out=t3[:, n0:n0 + 2, :, :, :].rearrange("p n h c j -> p (n h) c j"),
+                    in0=t12[:, 0, n0:n0 + 2, :, :, :].rearrange("p n h c j -> p (n h) c j"),
+                    in1=t12[:, 1, n0:n0 + 2, :, :, :].rearrange("p n h c j -> p (n h) c j")[:, :, ::-1, :],
+                    op=ALU.add,
+                )
+
+        def finish_pool(gi):
+            pg, b = order[gi]
+            st = state[gi]
+            st["oqk"] = deep.tile([P, NH, NT, DH], F32, tag="oqk", name="oqk")
+            n = NT - 1
+            for h in range(2):
+                nc.gpsimd.tensor_scalar(
+                    out=st["oqk"][:, h, n, :], in0=st["t3"][:, n, h, :, :].rearrange("p c j -> p (c j)"),
+                    scalar1=st["rinv"][:, n * NH + h:n * NH + h + 1], scalar2=0.0, op0=ALU.mult, op1=ALU.add,
+                )
+            nc.gpsimd.tensor_tensor(
+                out=st["oqk"][:, 0:2, n, :], in0=st["oqk"][:, 0:2, n, :],
+                in1=cq_tiles[pg][:].unsqueeze(1).to_broadcast([P, 2, DH]), op=ALU.add,
+            )
 
         def finish(gi, blocks):
             pg, b = order[gi]
@@ -312,7 +333,7 @@ def tile_groupqueryattention_pa_t_kernel(
             if "oqk" not in st:
                 st["oqk"] = deep.tile([P, NH, NT, DH], F32, tag="oqk", name="oqk")
             for n, h in blocks:
-                summed = st["t3"][:, n, h, :, :] if "t3" in st else st["t12"][:, n, 0, h, :, :]
+                summed = st["t3"][:, n, h, :, :] if "t3" in st else st["t12"][:, 0, n, h, :, :]
                 nc.vector.scalar_tensor_tensor(
                     out=st["oqk"][:, h, n, :],
                     in0=summed.rearrange("p c j -> p (c j)"),
@@ -345,6 +366,7 @@ def tile_groupqueryattention_pa_t_kernel(
 
         late_tables = {0: (2, 0), 1: (2, 1), 3: (2, 2), 4: (2, 3), 6: (3, 0), 7: (3, 1), 9: (3, 2), 10: (3, 3)}
         all_blocks = [(n, h) for n in range(NT) for h in range(NH)]
+        vector_blocks = [blk for blk in all_blocks if blk not in ((NT - 1, 0), (NT - 1, 1))]
 
         w_grouped = transpose_group(w_sb, share=True)
         for pg, n in ((0, 0), (0, 1), (1, 0), (1, 1)):
@@ -358,6 +380,7 @@ def tile_groupqueryattention_pa_t_kernel(
                 scaled = table_front(pg, n)
             if 0 <= it - 1 < NG - 1:
                 join_pool(it - 1)
+                finish_pool(it - 1)
             if it == 1 or it == 2:
                 table_tile(nc.gpsimd, 1, it + 1, it + 2)
             for n in range(NT):
@@ -365,17 +388,19 @@ def tile_groupqueryattention_pa_t_kernel(
                     products(it, n)
                 if 0 <= it + 1 < NG:
                     project(it + 1, n)
+                if it == NG - 1 and n == 1:
+                    join(nc.gpsimd, it, 0, 2)
             if 0 <= it + 1 < NG:
                 norm_root(it + 1)
             if it in late_tables:
                 pg, n = late_tables[it]
                 table_back(pg, n, scaled)
             if 0 <= it - 1 < NG - 1:
-                finish(it - 1, all_blocks[:-1])
+                finish(it - 1, vector_blocks[:-1])
             if it + 2 < NG:
                 quant(it + 2)
             if 0 <= it - 1 < NG - 1:
-                finish(it - 1, all_blocks[-1:])
+                finish(it - 1, vector_blocks[-1:])
                 store(it - 1, 0, NT)
                 pg, b = order[it - 1]
                 if b == B - 1 and pg + 1 < PG:
@@ -389,7 +414,7 @@ def tile_groupqueryattention_pa_t_kernel(
             if it == 2:
                 table_t(1)
             if it - 1 == NG - 1:
-                for n0 in (0, 2):
-                    join(nc.vector, it - 1, n0, n0 + 2)
+                join(nc.vector, it - 1, 2, NT)
+                for n0 in (2, 0):
                     finish(it - 1, all_blocks[n0 * NH:(n0 + 2) * NH])
                     store(it - 1, n0, n0 + 2)

@@ -62,15 +62,33 @@ def tile_groupqueryattention_pa_t_kernel(
 
         x_sb = []
         w_sb = const.tile([P, NT, D], BF16, name="w_sb")
-        vb = const.tile([P, 4, DH], BF16, name="vb")
+        vrow = const.tile([P, 4, DH], BF16, name="vrow")
+        nc.vector.memset(vrow[:], 0.0)
+        ones_b = const.tile([P, P], BF16, name="ones_b")
+        nc.vector.memset(ones_b[:], 1.0)
+        vectors = (q_scale, k_scale, q_shift, k_shift)
+
+        def load_vector(i):
+            nc.scalar.dma_start(out=vrow[0:1, i, :], in_=vectors[i].rearrange("(o j) -> o j", o=1))
+
+        def spread_vectors(i0):
+            spread = psum_t.tile([P, 2, DH], F32, tag="xt", name="spread")
+            nc.tensor.matmul(
+                spread[:].rearrange("p i j -> p (i j)"), lhsT=ones_b[:],
+                rhs=vrow[:, i0:i0 + 2, :].rearrange("p i j -> p (i j)"), start=True, stop=True,
+            )
+            return spread
+
         cs_sb = const.tile([P, 2, PG * NT, DH], BF16, name="cs_sb")
         nc.sync.dma_start(out=w_sb[:, 0:2, :], in_=wq.rearrange("(r p) k -> p r k", p=P))
         nc.sync.dma_start(out=w_sb[:, 2, :], in_=wk)
         nc.sync.dma_start(out=w_sb[:, 3, :], in_=wv)
         load_x(0)
+        load_vector(0)
+        load_vector(1)
         load_cs(nc.scalar, 0)
-        for i, vec in enumerate((q_scale, k_scale, q_shift, k_shift)):
-            nc.scalar.dma_start(out=vb[:, i, :], in_=vec.partition_broadcast(P))
+        load_vector(2)
+        load_vector(3)
         load_x(1)
         load_cs(nc.sync, 1)
         load_x(2)
@@ -94,14 +112,16 @@ def tile_groupqueryattention_pa_t_kernel(
         nc.vector.tensor_copy(out=perm_f[:, HALF:], in_=ident_f[:, 0:HALF])
 
         g3 = const.tile([P, NH, DH], F32, name="g3")
-        nc.vector.tensor_scalar_add(out=g3[:, 0:2, :], in0=vb[:, 0:1, :].to_broadcast([P, 2, DH]), scalar1=1.0)
-        nc.vector.tensor_scalar_add(out=g3[:, 2, :], in0=vb[:, 1, :], scalar1=1.0)
+        scales_ps = spread_vectors(0)
+        nc.vector.tensor_scalar_add(out=g3[:, 0:2, :], in0=scales_ps[:, 0:1, :].to_broadcast([P, 2, DH]), scalar1=1.0)
+        nc.vector.tensor_scalar_add(out=g3[:, 2, :], in0=scales_ps[:, 1, :], scalar1=1.0)
         gs3 = const.tile([P, NH, DH], F32, name="gs3")
         nc.vector.tensor_copy(out=gs3[:, :, 0:HALF], in_=g3[:, :, 0:HALF])
         nc.vector.tensor_scalar_mul(out=gs3[:, :, HALF:], in0=g3[:, :, HALF:], scalar1=-1.0)
 
         dc = const.tile([P, 2, DH], BF16, name="dc")
         ds = const.tile([P, 2, DH], BF16, name="ds")
+        dg = const.tile([P, 2, 2, DH], F32, name="dg")
         bsrc = const.tile([P, 4, DH], F32, name="bsrc")
         colv = const.tile([P, 4], F32, name="colv")
 
@@ -110,21 +130,27 @@ def tile_groupqueryattention_pa_t_kernel(
         nc.vector.tensor_copy(out=bsrc[:, 2:4, HALF:], in_=gs3[:, 1:3, 0:HALF])
 
         def small_tables():
+            shifts_ps = spread_vectors(2)
             nc.vector.tensor_tensor(
-                out=dc[:], in0=vb[:, 2:4, :], in1=ident_b[:].unsqueeze(1).to_broadcast([P, 2, DH]), op=ALU.mult
+                out=dc[:], in0=shifts_ps[:], in1=ident_b[:].unsqueeze(1).to_broadcast([P, 2, DH]), op=ALU.mult
             )
             nc.vector.scalar_tensor_tensor(
-                out=ds[:, :, 0:HALF], in0=vb[:, 2:4, HALF:], scalar=-1.0,
+                out=ds[:, :, 0:HALF], in0=shifts_ps[:, :, HALF:], scalar=-1.0,
                 in1=ident_b[:, 0:HALF].unsqueeze(1).to_broadcast([P, 2, HALF]), op0=ALU.mult, op1=ALU.mult,
             )
             nc.vector.tensor_tensor(
-                out=ds[:, :, HALF:], in0=vb[:, 2:4, 0:HALF],
+                out=ds[:, :, HALF:], in0=shifts_ps[:, :, 0:HALF],
                 in1=ident_b[:, HALF:].unsqueeze(1).to_broadcast([P, 2, HALF]), op=ALU.mult,
             )
             col_ps = psum_t.tile([P, 4, P], F32, tag="xt", name="col_ps")
             for i in range(4):
                 nc.tensor.transpose(col_ps[:, i, :], bsrc[:, i, :], ident_f[:])
             nc.scalar.copy(out=colv[:], in_=col_ps[:, :, 0])
+            for i in range(4):
+                nc.scalar.activation(
+                    out=dg[:, i // 2, i % 2, :], in_=ident_f[:] if i < 2 else perm_f[:], func=ACT.Copy,
+                    scale=colv[:, i:i + 1],
+                )
 
         NG = len(order)
         w_codes = const.tile([P, NT * P], U32, name="w_codes", align_bytes=64)
@@ -217,18 +243,17 @@ def tile_groupqueryattention_pa_t_kernel(
             for c in range(2):
                 nc.tensor.transpose(cs_ps[:, c, :], cs_sb[:, c, pg * NT + n, :], ident_b[:])
             nc.scalar.copy(out=cst_tiles[pg][:, :, n, :], in_=cs_ps[:])
-            xs4 = work.tile([P, 4, P], F32, tag="xs4", name="xs4")
-            for i in range(4):
-                nc.scalar.activation(
-                    out=xs4[:, i, :], in_=cs_ps[:, i // 2, :], func=ACT.Copy, scale=colv[:, i:i + 1]
-                )
-            return xs4
+            csf = work.tile([P, 2, P], F32, tag="csf", name="csf")
+            nc.scalar.copy(out=csf[:], in_=cs_ps[:])
+            return csf
 
-        def table_back(pg, n, xs4):
+        def table_back(pg, n, csf):
             gt = psum_t.tile([P, 2, 2, P], F32, tag="xt", name="gt")
             for a in range(2):
-                for qk in range(2):
-                    nc.tensor.transpose(gt[:, a, qk, :], xs4[:, 2 * a + qk, :], ident_f[:] if a == 0 else perm_f[:])
+                nc.tensor.matmul(
+                    gt[:, a, :, :].rearrange("p q j -> p (q j)"), lhsT=csf[:, a, :],
+                    rhs=dg[:, a, :, :].rearrange("p q j -> p (q j)"), start=True, stop=True,
+                )
             g12 = g12_tiles[pg]
             nc.scalar.copy(out=g12[:, n, :, 0:2, :], in_=gt[:, :, 0:1, :].to_broadcast([P, 2, 2, DH]))
             nc.scalar.copy(out=g12[:, n, :, 2, :], in_=gt[:, :, 1, :])
@@ -377,10 +402,11 @@ def tile_groupqueryattention_pa_t_kernel(
                 front(it + 2)
             if it in late_tables:
                 pg, n = late_tables[it]
-                scaled = table_front(pg, n)
+                wide = table_front(pg, n)
             if 0 <= it - 1 < NG - 1:
                 join_pool(it - 1)
-                finish_pool(it - 1)
+                if it - 1 >= 2:
+                    finish_pool(it - 1)
             if it == 1 or it == 2:
                 table_tile(nc.gpsimd, 1, it + 1, it + 2)
             for n in range(NT):
@@ -394,9 +420,9 @@ def tile_groupqueryattention_pa_t_kernel(
                 norm_root(it + 1)
             if it in late_tables:
                 pg, n = late_tables[it]
-                table_back(pg, n, scaled)
+                table_back(pg, n, wide)
             if 0 <= it - 1 < NG - 1:
-                finish(it - 1, vector_blocks[:-1])
+                finish(it - 1, (vector_blocks if it - 1 >= 2 else all_blocks)[:-1])
             if it + 2 < NG:
                 quant(it + 2)
             if 0 <= it - 1 < NG - 1:

from contextlib import ExitStack

import concourse.mybir as mybir
from concourse.masks import make_identity

F32 = mybir.dt.float32
BF16 = mybir.dt.bfloat16
U32 = mybir.dt.uint32
U8 = mybir.dt.uint8
FP8X4 = mybir.dt.float8_e4m3fn_x4
ALU = mybir.AluOpType
ACT = mybir.ActivationFunctionType

B, S, D = 4, 2048, 512
P = 128
DH = 128
HALF = DH // 2
NT = 4
GROUP = P * NT
PG = S // GROUP
NH = 3
EPS = 1e-6
FLOPS = 2 * B * S * D * 512


def tile_groupqueryattention_pa_t_kernel(
    tc, x, sin_thetas, cos_thetas, wq, wk, wv, q_scale, q_shift, k_scale, k_shift, out_0, out_1, out_2
):
    nc = tc.nc
    with ExitStack() as ctx:
        const = ctx.enter_context(tc.tile_pool(name="const", bufs=1))
        xpool = ctx.enter_context(tc.tile_pool(name="xpool", bufs=1))
        tabs = ctx.enter_context(tc.tile_pool(name="tabs", bufs=1))
        work = ctx.enter_context(tc.tile_pool(name="work", bufs=2))
        deep = ctx.enter_context(tc.tile_pool(name="deep", bufs=3))
        single = ctx.enter_context(tc.tile_pool(name="single", bufs=1))
        psum_t = ctx.enter_context(tc.psum_pool(name="psum_t", bufs=2))
        psum_u = ctx.enter_context(tc.psum_pool(name="psum_u", bufs=4))
        psum_c = ctx.enter_context(tc.psum_pool(name="psum_c", bufs=2))
        ctx.enter_context(tc.manual_schedule())

        order = [(pg, b) for pg in range(PG) for b in range(B)]

        ident_f = const.tile([P, P], F32, name="ident_f")
        make_identity(nc, ident_f[:])

        def load_x(gi):
            pg, b = order[gi]
            xs = xpool.tile([P, NT, D], BF16, name="xs%d" % gi)
            nc.sync.dma_start(
                out=xs[:].rearrange("p n k -> p (n k)"),
                in_=x[b, pg * GROUP:(pg + 1) * GROUP, :].rearrange("(p n) k -> p (n k)", n=NT),
            )
            x_sb.append(xs)

        def load_cs(eng, pg):
            for c, tab in enumerate((cos_thetas, sin_thetas)):
                eng.dma_start(
                    out=cs_sb[:, c, pg * NT:(pg + 1) * NT, :],
                    in_=tab[pg * GROUP:(pg + 1) * GROUP, :].rearrange("(p n) j -> p n j", n=NT),
                )

        x_sb = []
        w_sb = const.tile([P, NT, D], BF16, name="w_sb")
        vrow = const.tile([P, 4, DH], BF16, name="vrow")
        nc.vector.memset(vrow[:], 0.0)
        ones_b = const.tile([P, P], BF16, name="ones_b")
        nc.vector.memset(ones_b[:], 1.0)
        vectors = (q_scale, k_scale, q_shift, k_shift)

        def load_vector(i):
            nc.scalar.dma_start(out=vrow[0:1, i, :], in_=vectors[i].rearrange("(o j) -> o j", o=1))

        def spread_vectors(i0):
            spread = psum_t.tile([P, 2, DH], F32, tag="xt", name="spread")
            nc.tensor.matmul(
                spread[:].rearrange("p i j -> p (i j)"), lhsT=ones_b[:],
                rhs=vrow[:, i0:i0 + 2, :].rearrange("p i j -> p (i j)"), start=True, stop=True,
            )
            return spread

        cs_sb = const.tile([P, 2, PG * NT, DH], BF16, name="cs_sb")
        nc.sync.dma_start(out=w_sb[:, 0:2, :], in_=wq.rearrange("(r p) k -> p r k", p=P))
        nc.sync.dma_start(out=w_sb[:, 2, :], in_=wk)
        nc.sync.dma_start(out=w_sb[:, 3, :], in_=wv)
        load_x(0)
        load_vector(0)
        load_vector(1)
        load_cs(nc.scalar, 0)
        load_vector(2)
        load_vector(3)
        load_x(1)
        load_cs(nc.sync, 1)
        load_x(2)
        load_x(3)
        load_cs(nc.sync, 2)
        load_x(4)
        load_x(5)
        load_cs(nc.sync, 3)
        for gi in range(6, len(order)):
            load_x(gi)

        eps_t = const.tile([P, 1], F32, name="eps_t")
        nc.vector.memset(eps_t[:], EPS)
        warm = const.tile([P, 1], F32, name="warm")
        nc.scalar.activation(out=warm[:], in_=eps_t[:], func=ACT.Abs_reciprocal_sqrt)

        ident_b = const.tile([P, P], BF16, name="ident_b")
        nc.vector.tensor_copy(out=ident_b[:], in_=ident_f[:])
        perm_f = const.tile([P, P], F32, name="perm_f")
        nc.vector.tensor_copy(out=perm_f[:, 0:HALF], in_=ident_f[:, HALF:])
        nc.vector.tensor_copy(out=perm_f[:, HALF:], in_=ident_f[:, 0:HALF])

        g3 = const.tile([P, NH, DH], F32, name="g3")
        scales_ps = spread_vectors(0)
        nc.vector.tensor_scalar_add(out=g3[:, 0:2, :], in0=scales_ps[:, 0:1, :].to_broadcast([P, 2, DH]), scalar1=1.0)
        nc.vector.tensor_scalar_add(out=g3[:, 2, :], in0=scales_ps[:, 1, :], scalar1=1.0)
        gs3 = const.tile([P, NH, DH], F32, name="gs3")
        nc.vector.tensor_copy(out=gs3[:, :, 0:HALF], in_=g3[:, :, 0:HALF])
        nc.vector.tensor_scalar_mul(out=gs3[:, :, HALF:], in0=g3[:, :, HALF:], scalar1=-1.0)

        dc = const.tile([P, 2, DH], BF16, name="dc")
        ds = const.tile([P, 2, DH], BF16, name="ds")
        dg = const.tile([P, 2, 2, DH], F32, name="dg")
        bsrc = const.tile([P, 4, DH], F32, name="bsrc")
        colv = const.tile([P, 4], F32, name="colv")

        nc.vector.tensor_copy(out=bsrc[:, 0:2, :], in_=g3[:, 1:3, :])
        nc.vector.tensor_copy(out=bsrc[:, 2:4, 0:HALF], in_=gs3[:, 1:3, HALF:])
        nc.vector.tensor_copy(out=bsrc[:, 2:4, HALF:], in_=gs3[:, 1:3, 0:HALF])

        def small_tables():
            shifts_ps = spread_vectors(2)
            nc.vector.tensor_tensor(
                out=dc[:], in0=shifts_ps[:], in1=ident_b[:].unsqueeze(1).to_broadcast([P, 2, DH]), op=ALU.mult
            )
            nc.vector.scalar_tensor_tensor(
                out=ds[:, :, 0:HALF], in0=shifts_ps[:, :, HALF:], scalar=-1.0,
                in1=ident_b[:, 0:HALF].unsqueeze(1).to_broadcast([P, 2, HALF]), op0=ALU.mult, op1=ALU.mult,
            )
            nc.vector.tensor_tensor(
                out=ds[:, :, HALF:], in0=shifts_ps[:, :, 0:HALF],
                in1=ident_b[:, HALF:].unsqueeze(1).to_broadcast([P, 2, HALF]), op=ALU.mult,
            )
            col_ps = psum_t.tile([P, 4, P], F32, tag="xt", name="col_ps")
            for i in range(4):
                nc.tensor.transpose(col_ps[:, i, :], bsrc[:, i, :], ident_f[:])
            nc.scalar.copy(out=colv[:], in_=col_ps[:, :, 0])
            for i in range(4):
                nc.scalar.activation(
                    out=dg[:, i // 2, i % 2, :], in_=ident_f[:] if i < 2 else perm_f[:], func=ACT.Copy,
                    scale=colv[:, i:i + 1],
                )

        NG = len(order)
        w_codes = const.tile([P, NT * P], U32, name="w_codes", align_bytes=64)
        w_scales = const.tile([P, NT * P], U8, name="w_scales", align_bytes=64)
        state = {}
        g12_tiles = {}
        cst_tiles = {}
        c_tiles = {}
        cq_tiles = {}

        def transpose_group(src, share=False):
            grouped = work.tile([P, NT, P, 4], BF16, tag="grouped", name="grouped", align_bytes=64)
            gwords = grouped[:].bitcast(F32)
            banks = []
            for half in range(2):
                xt = psum_t.tile([P, 2, 2, P], F32, tag="xt", name="xt")
                for i in range(2):
                    words = src[:, 2 * half + i, :].bitcast(F32)
                    for u in range(2):
                        nc.tensor.transpose(xt[:, i, u, :], words[:, u * P:(u + 1) * P], ident_f[:])
                banks.append(xt)
            for half in range(2):
                dst = gwords[:, 2 * half:2 * half + 2, :, :]
                if share and half == 1:
                    nc.vector.tensor_copy(out=dst, in_=banks[half][:].rearrange("p i u r -> p i r u"))
                else:
                    nc.scalar.copy(out=dst, in_=banks[half][:].rearrange("p i u r -> p i r u"))
            return grouped

        def quantise(grouped, codes, scales):
            nc.vector.quantize_mx(
                out=codes[:].bitcast(FP8X4), scales=scales[:], in_=grouped[:].rearrange("p n r t -> p (n r t)")
            )

        def table_g1(eng, pg, n0, n1):
            g12 = g12_tiles[pg]
            k = n1 - n0
            cosv = cs_sb[:, 0, pg * NT + n0:pg * NT + n1, :]
            eng.tensor_tensor(
                out=g12[:, n0:n1, 0, :, :], in0=cosv.unsqueeze(2).to_broadcast([P, k, NH, DH]),
                in1=g3[:].unsqueeze(1).to_broadcast([P, k, NH, DH]), op=ALU.mult,
            )

        def table_g2(eng, pg, n0, n1, c):
            g12 = g12_tiles[pg]
            k = n1 - n0
            sinv = cs_sb[:, 1, pg * NT + n0:pg * NT + n1, (1 - c) * HALF:(2 - c) * HALF]
            eng.tensor_tensor(
                out=g12[:, n0:n1, 1, :, c * HALF:(c + 1) * HALF],
                in0=sinv.unsqueeze(2).to_broadcast([P, k, NH, HALF]),
                in1=gs3[:, :, c * HALF:(c + 1) * HALF].unsqueeze(1).to_broadcast([P, k, NH, HALF]), op=ALU.mult,
            )

        def table_t(pg):
            cst_ps = psum_t.tile([P, 2, NT, P], BF16, tag="xt", name="cst_ps")
            for c in range(2):
                for n in range(NT):
                    nc.tensor.transpose(cst_ps[:, c, n, :], cs_sb[:, c, pg * NT + n, :], ident_b[:])
            cst = work.tile([P, 2, NT, P], BF16, tag="cst", name="cst")
            nc.scalar.copy(out=cst[:], in_=cst_ps[:])
            cst_tiles[pg] = cst

        def table_c(pg):
            cst = cst_tiles[pg]
            pair = []
            for half in range(2):
                c_ps = psum_c.tile([P, 2, 2, DH], F32, tag="c", name="c_ps")
                for i in range(2):
                    n = 2 * half + i
                    dst = c_ps[:, i, :, :].rearrange("p a j -> p (a j)")
                    nc.tensor.matmul(
                        dst, lhsT=cst[:, 0, n, :], rhs=dc[:].rearrange("p a j -> p (a j)"), start=True, stop=False
                    )
                    nc.tensor.matmul(
                        dst, lhsT=cst[:, 1, n, :], rhs=ds[:].rearrange("p a j -> p (a j)"), start=False, stop=True
                    )
                pair.append(c_ps)
            c_tiles[pg] = pair
            cq_last = const.tile([P, DH], F32, name="cq_last%d" % pg)
            nc.scalar.copy(out=cq_last[:], in_=pair[1][:, 1, 0, :])
            cq_tiles[pg] = cq_last

        def front(gi):
            state[gi] = {"grouped": transpose_group(x_sb[gi], share=(gi < 2))}

        def table_front(pg, n):
            if n == 0:
                cst_tiles[pg] = work.tile([P, 2, NT, P], BF16, tag="cst", name="cst")
            cs_ps = psum_t.tile([P, 2, P], BF16, tag="xt", name="cs_ps")
            for c in range(2):
                nc.tensor.transpose(cs_ps[:, c, :], cs_sb[:, c, pg * NT + n, :], ident_b[:])
            nc.scalar.copy(out=cst_tiles[pg][:, :, n, :], in_=cs_ps[:])
            csf = work.tile([P, 2, P], F32, tag="csf", name="csf")
            nc.scalar.copy(out=csf[:], in_=cs_ps[:])
            return csf

        def table_back(pg, n, csf):
            gt = psum_t.tile([P, 2, 2, P], F32, tag="xt", name="gt")
            for a in range(2):
                nc.tensor.matmul(
                    gt[:, a, :, :].rearrange("p q j -> p (q j)"), lhsT=csf[:, a, :],
                    rhs=dg[:, a, :, :].rearrange("p q j -> p (q j)"), start=True, stop=True,
                )
            g12 = g12_tiles[pg]
            nc.scalar.copy(out=g12[:, n, :, 0:2, :], in_=gt[:, :, 0:1, :].to_broadcast([P, 2, 2, DH]))
            nc.scalar.copy(out=g12[:, n, :, 2, :], in_=gt[:, :, 1, :])

        def quant(gi):
            st = state[gi]
            st["codes"] = deep.tile([P, NT * P], U32, tag="codes", name="codes", align_bytes=64)
            st["scales"] = deep.tile([P, NT * P], U8, tag="scales", name="scales", align_bytes=64)
            quantise(st["grouped"], st["codes"], st["scales"])

        def project(gi, n):
            st = state[gi]
            if n == 0:
                st["ss"] = deep.tile([P, NT * NH], F32, tag="ss", name="ss")
                st["ov"] = deep.tile([P, NT, DH], F32, tag="ov", name="ov")
                st["u"] = []
            codes, scales, ss, ov = st["codes"], st["scales"], st["ss"], st["ov"]
            u = psum_u.tile([P, 4 * DH], F32, tag="u", name="u")
            st["u"].append(u)
            nc.tensor.matmul_mx(
                out=u[:],
                lhsT=codes[:, n * P:(n + 1) * P].bitcast(FP8X4),
                lhsT_scale=scales[:, n * P:(n + 1) * P],
                rhs=w_codes[:].bitcast(FP8X4),
                rhs_scale=w_scales[:],
                start=True,
                stop=True,
            )
            for h in range(NH):
                junk = work.tile([P, DH], BF16, tag="junk", name="junk")
                nc.scalar.activation(
                    out=junk[:], in_=u[:, h * DH:(h + 1) * DH], func=ACT.Square,
                    accum_out=ss[:, n * NH + h:n * NH + h + 1],
                )
            nc.scalar.copy(out=ov[:, n, :], in_=u[:, NH * DH:])

        def norm_root(gi):
            pg, b = order[gi]
            st = state[gi]
            st["rinv"] = deep.tile([P, NT * NH], F32, tag="rinv", name="rinv")
            nc.scalar.activation(
                out=st["rinv"][:], in_=st["ss"][:], func=ACT.Abs_reciprocal_sqrt, scale=1.0 / DH, bias=eps_t[:]
            )
            lo = pg * GROUP
            nc.sync.dma_start(
                out=out_2[b, 0, lo:lo + GROUP, :].rearrange("(p n) j -> p (n j)", n=NT),
                in_=st["ov"][:].rearrange("p n j -> p (n j)"),
            )

        def products(gi, n):
            pg, b = order[gi]
            st = state[gi]
            if n == 0:
                st["t12"] = deep.tile([P, 2, NT, NH, 2, HALF], F32, tag="t12", name="t12")
            u = st["u"][n]
            nc.vector.tensor_tensor(
                out=st["t12"][:, :, n, :, :, :].rearrange("p a h c j -> p a (h c j)"),
                in0=u[:, 0:NH * DH].unsqueeze(1).to_broadcast([P, 2, NH * DH]),
                in1=g12_tiles[pg][:, n, :, :, :].rearrange("p a h j -> p a (h j)"),
                op=ALU.mult,
            )

        def join(eng, gi, n0, n1):
            t12 = state[gi]["t12"]
            for c in range(2):
                eng.tensor_tensor(
                    out=t12[:, 0, n0:n1, :, c, :], in0=t12[:, 0, n0:n1, :, c, :],
                    in1=t12[:, 1, n0:n1, :, 1 - c, :], op=ALU.add,
                )

        def join_pool(gi):
            st = state[gi]
            t12 = st["t12"]
            t3 = single.tile([P, NT, NH, 2, HALF], F32, tag="t3", name="t3")
            st["t3"] = t3
            for n0 in (0, 2):
                nc.gpsimd.tensor_tensor(
                    out=t3[:, n0:n0 + 2, :, :, :].rearrange("p n h c j -> p (n h) c j"),
                    in0=t12[:, 0, n0:n0 + 2, :, :, :].rearrange("p n h c j -> p (n h) c j"),
                    in1=t12[:, 1, n0:n0 + 2, :, :, :].rearrange("p n h c j -> p (n h) c j")[:, :, ::-1, :],
                    op=ALU.add,
                )

        def finish_pool(gi):
            pg, b = order[gi]
            st = state[gi]
            st["oqk"] = deep.tile([P, NH, NT, DH], F32, tag="oqk", name="oqk")
            n = NT - 1
            for h in range(2):
                nc.gpsimd.tensor_scalar(
                    out=st["oqk"][:, h, n, :], in0=st["t3"][:, n, h, :, :].rearrange("p c j -> p (c j)"),
                    scalar1=st["rinv"][:, n * NH + h:n * NH + h + 1], scalar2=0.0, op0=ALU.mult, op1=ALU.add,
                )
            nc.gpsimd.tensor_tensor(
                out=st["oqk"][:, 0:2, n, :], in0=st["oqk"][:, 0:2, n, :],
                in1=cq_tiles[pg][:].unsqueeze(1).to_broadcast([P, 2, DH]), op=ALU.add,
            )

        def finish(gi, blocks):
            pg, b = order[gi]
            st = state[gi]
            if "oqk" not in st:
                st["oqk"] = deep.tile([P, NH, NT, DH], F32, tag="oqk", name="oqk")
            for n, h in blocks:
                summed = st["t3"][:, n, h, :, :] if "t3" in st else st["t12"][:, 0, n, h, :, :]
                nc.vector.scalar_tensor_tensor(
                    out=st["oqk"][:, h, n, :],
                    in0=summed.rearrange("p c j -> p (c j)"),
                    scalar=st["rinv"][:, n * NH + h:n * NH + h + 1],
                    in1=c_tiles[pg][n // 2][:, n % 2, h // 2, :],
                    op0=ALU.mult,
                    op1=ALU.add,
                )

        def store(gi, n0, n1):
            pg, b = order[gi]
            oqk = state[gi]["oqk"]
            lo = pg * GROUP
            nc.sync.dma_start(
                out=out_0[b, :, lo:lo + GROUP, :].rearrange("h (p n) j -> p h n j", n=NT)[:, :, n0:n1, :],
                in_=oqk[:, 0:2, n0:n1, :],
            )
            nc.sync.dma_start(
                out=out_1[b, 0, lo:lo + GROUP, :].rearrange("(p n) j -> p n j", n=NT)[:, n0:n1, :],
                in_=oqk[:, 2, n0:n1, :],
            )

        for pg in range(PG):
            g12_tiles[pg] = tabs.tile([P, NT, 2, NH, DH], F32, name="g12_%d" % pg)

        def table_tile(eng, pg, n0, n1):
            table_g1(eng, pg, n0, n1)
            table_g2(eng, pg, n0, n1, 0)
            table_g2(eng, pg, n0, n1, 1)

        late_tables = {0: (2, 0), 1: (2, 1), 3: (2, 2), 4: (2, 3), 6: (3, 0), 7: (3, 1), 9: (3, 2), 10: (3, 3)}
        all_blocks = [(n, h) for n in range(NT) for h in range(NH)]
        vector_blocks = [blk for blk in all_blocks if blk not in ((NT - 1, 0), (NT - 1, 1))]

        w_grouped = transpose_group(w_sb, share=True)
        for pg, n in ((0, 0), (0, 1), (1, 0), (1, 1)):
            table_tile(nc.gpsimd, pg, n, n + 1)
        quantise(w_grouped, w_codes, w_scales)
        for it in range(-2, NG + 1):
            if it + 2 < NG:
                front(it + 2)
            if it in late_tables:
                pg, n = late_tables[it]
                wide = table_front(pg, n)
            if 0 <= it - 1 < NG - 1:
                join_pool(it - 1)
                if it - 1 >= 2:
                    finish_pool(it - 1)
            if it == 1 or it == 2:
                table_tile(nc.gpsimd, 1, it + 1, it + 2)
            for n in range(NT):
                if 0 <= it < NG:
                    products(it, n)
                if 0 <= it + 1 < NG:
                    project(it + 1, n)
                if it == NG - 1 and n == 1:
                    join(nc.gpsimd, it, 0, 2)
            if 0 <= it + 1 < NG:
                norm_root(it + 1)
            if it in late_tables:
                pg, n = late_tables[it]
                table_back(pg, n, wide)
            if 0 <= it - 1 < NG - 1:
                finish(it - 1, (vector_blocks if it - 1 >= 2 else all_blocks)[:-1])
            if it + 2 < NG:
                quant(it + 2)
            if 0 <= it - 1 < NG - 1:
                finish(it - 1, vector_blocks[-1:])
                store(it - 1, 0, NT)
                pg, b = order[it - 1]
                if b == B - 1 and pg + 1 < PG:
                    table_c(pg + 1)
            if it < 0:
                table_tile(nc.vector, 0, it + NT, it + NT + 1)
            if it == -1:
                small_tables()
                table_t(0)
                table_c(0)
            if it == 2:
                table_t(1)
            if it - 1 == NG - 1:
                join(nc.vector, it - 1, 2, NT)
                for n0 in (2, 0):
                    finish(it - 1, all_blocks[n0 * NH:(n0 + 2) * NH])
                    store(it - 1, n0, n0 + 2)
